import numpy as np
import ml_dtypes


def mxq(x, axis, fmt="e4m3"):
    dtype, down = {"e4m3": (ml_dtypes.float8_e4m3fn, 7), "e5m2": (ml_dtypes.float8_e5m2, 14)}[fmt]
    v = np.moveaxis(np.asarray(x, np.float32).astype(ml_dtypes.bfloat16).astype(np.float64), axis, -1)
    blocks = v.reshape(v.shape[:-1] + (-1, 32))
    amax = np.abs(blocks).max(-1, keepdims=True)
    byte = np.maximum(np.where(amax > 0, np.frexp(amax)[1] - 1 + 127, 0) - down, 1)
    scale = np.exp2(byte - 127.0)
    codes = (blocks / scale).astype(np.float32).astype(dtype).astype(np.float64)
    return np.moveaxis((codes * scale).reshape(v.shape), -1, axis)


WIDE = False


def mx_kscale(k):
    if not WIDE:
        return np.ones(k)
    levels = np.array([10, -10, 5, -5, 0])
    if k % 512:
        return np.exp2(np.random.permutation(np.resize(levels, k // 32))).repeat(32)
    a = np.empty((k // 512, 16))
    for p in range(k // 512):
        a[p, :8] = np.random.permutation(np.resize(levels, 8))
        for g in range(8):
            far = levels[np.abs(levels - a[p, g]) >= 10]
            a[p, g + 8] = far[np.random.randint(len(far))]
    return np.exp2(a.ravel()).repeat(32)


BF16 = ml_dtypes.bfloat16


def bf(x):
    return np.asarray(x, np.float32).astype(BF16)


def f64(x):
    return np.asarray(x).astype(np.float64)


N, IN_F, OUT_F = 1024, 512, 512
POW = 2


def setup_inputs():
    s = mx_kscale(IN_F)
    u = np.exp2(np.round(np.log2(mx_kscale(N)) / 2))
    return {"input": bf(np.random.standard_normal((N, IN_F)) * s / (u * u)[:, None]),
            "adj": bf(np.random.uniform(0.0, 1.0, (N, N)) * 1.5 / N ** 0.25 * u),
            "weight": bf(np.random.uniform(-1.0, 1.0, (IN_F, OUT_F)) * 1.7 / np.sqrt(IN_F) / s[:, None]),
            "bias": bf(np.random.standard_normal(OUT_F) * 0.3)}


def reference(input, adj, weight, bias):
    k_adj = f64(adj) ** POW
    support = f64(bf(mxq(f64(input), 1, "e4m3") @ mxq(f64(weight), 0, "e4m3")))
    out = (mxq(k_adj, 1, "e4m3") @ mxq(support, 0, "e4m3")) + f64(bias)
    return np.where(out > 0, out, np.expm1(out))

@@ -1,0 +1,273 @@
+from contextlib import ExitStack
+
+import concourse.mybir as mybir
+from concourse.masks import make_identity
+
+FLOPS = 2 * 1024 * 512 * 512 + 2 * 1024 * 1024 * 512
+
+F32 = mybir.dt.float32
+BF16 = mybir.dt.bfloat16
+U32 = mybir.dt.uint32
+U8 = mybir.dt.uint8
+FP8X4 = mybir.dt.float8_e4m3fn_x4
+ALU = mybir.AluOpType
+ACT = mybir.ActivationFunctionType
+
+P = 128
+NODES = 1024
+FEAT = 512
+OUTF = 512
+MANUAL = True
+AHEAD = 3
+NWARM = 6
+MIN_ON_SCALAR = (5, 6)
+SPLIT_TILES = (7,)
+SC_ON_VECTOR = (1, 3)
+BANK_DT = BF16
+
+
+def tile_netgraphconvolution_kernel(tc, x, adj, weight, bias, out):
+    nc = tc.nc
+    with ExitStack() as ctx:
+        keep = ctx.enter_context(tc.tile_pool(name="keep", bufs=1))
+        psum = ctx.enter_context(tc.psum_pool(name="psum", bufs=8))
+        if MANUAL:
+            ctx.enter_context(tc.manual_schedule())
+
+        bias_row = keep.tile([P, OUTF], BF16, name="bias_row", tag="bias_row")
+        ones = keep.tile([P, P], BF16, name="ones", tag="ones")
+        warm = keep.tile([P, 8], F32, name="warm", tag="warm")
+        zeros = keep.tile([P, OUTF], BF16, name="zeros", tag="zeros")
+        nc.vector.memset(warm[:], 0.0)
+        nc.vector.memset(ones[:], 1.0)
+        nc.vector.memset(zeros[:], 0.0)
+        nc.vector.memset(bias_row[:], 0.0)
+        nc.scalar.activation(out=warm[:, 4:8], in_=warm[:, 0:4], func=ACT.Exp)
+        nc.scalar.dma_start(out=bias_row[0:1, :], in_=bias.rearrange("(a o) -> a o", a=1))
+
+        w_raw = keep.tile([P, 4, OUTF], BF16, name="w_raw", tag="w_raw")
+        nc.sync.dma_start(out=w_raw[:], in_=weight.rearrange("(p j) o -> p j o", j=4))
+        x_view = x.rearrange("(u m s) f -> u m s f", m=P, s=4)
+        x_raw = []
+        for u in range(4):
+            t = keep.tile([P, 2, FEAT], BF16, name="x_raw%d" % u, tag="x_raw%d" % u)
+            g, h = divmod(u, 2)
+            nc.sync.dma_start(out=t[:], in_=x_view[g, :, 2 * h : 2 * h + 2, :])
+            x_raw.append(t)
+        a_raw = []
+        for i in range(8):
+            t = keep.tile([P, NODES], BF16, name="a_raw%d" % i, tag="a_raw%d" % i)
+            nc.sync.dma_start(out=t[:], in_=adj[i * P : (i + 1) * P, :])
+            a_raw.append(t)
+
+        ident = keep.tile([P, P], F32, name="ident", tag="ident")
+        make_identity(nc, ident[:])
+        bank_w = psum.tile([P, OUTF], F32, name="bank_w", tag="bank")
+        for n in range(NWARM):
+            nc.tensor.matmul(out=bank_w[:], lhsT=ones[:], rhs=zeros[:], start=True, stop=True)
+
+        w_grp = keep.tile([P, OUTF, 4], BF16, name="w_grp", tag="w_grp", align_bytes=64)
+        w_codes = keep.tile([P, OUTF], U32, name="w_codes", tag="w_codes", align_bytes=64)
+        w_scales = keep.tile([P, OUTF], U8, name="w_scales", tag="w_scales", align_bytes=64)
+        HALF = OUTF // 2
+        for c in range(2):
+            cols = slice(c * HALF, (c + 1) * HALF)
+            nc.vector.tensor_copy(out=w_grp[:, cols, :], in_=w_raw[:, :, cols].rearrange("p j o -> p o j"))
+        for c in range(2):
+            cols = slice(c * HALF, (c + 1) * HALF)
+            nc.vector.quantize_mx(
+                out=w_codes[:, cols].bitcast(FP8X4),
+                scales=w_scales[:, cols],
+                in_=w_grp[:, cols, :].rearrange("p o j -> p (o j)"),
+            )
+
+        x_codes = []
+        x_scales = []
+        x_grp = []
+
+        def x_turn(u):
+            bank = psum.tile([P, 512], F32, name="bank_x%d" % u, tag="bank")
+            for s in range(2):
+                words = x_raw[u][:, s, :].bitcast(F32)
+                for e in range(2):
+                    c0 = e * 256 + s * P
+                    nc.tensor.transpose(out=bank[:, c0 : c0 + P], in_=words[:, e:256:2], identity=ident[:])
+            grp = keep.tile([P, 1024], BF16, name="x_grp%d" % u, tag="x_grp%d" % u, align_bytes=64)
+            nc.scalar.copy(
+                out=grp[:].bitcast(F32).rearrange("p (q e) -> p q e", e=2),
+                in_=bank[:].rearrange("p (e q) -> p q e", e=2),
+            )
+            x_grp.append(grp)
+
+        def x_quant(u):
+            codes = keep.tile([P, 256], U32, name="x_codes%d" % u, tag="x_codes%d" % u, align_bytes=64)
+            scales = keep.tile([P, 256], U8, name="x_scales%d" % u, tag="x_scales%d" % u, align_bytes=64)
+            nc.vector.quantize_mx(out=codes[:].bitcast(FP8X4), scales=scales[:], in_=x_grp[u][:])
+            x_codes.append(codes)
+            x_scales.append(scales)
+
+        for u in range(4):
+            x_turn(u)
+            x_quant(u)
+
+
+        k_grp = {}
+        k_codes = {}
+        k_scales = {}
+
+        def a_turn(i):
+            bank = psum.tile([P, 512], F32, name="bank_a%d" % i, tag="bank")
+            words = a_raw[i][:].bitcast(F32)
+            for g in range(2):
+                for e in range(2):
+                    c0 = e * 256 + g * P
+                    nc.tensor.transpose(
+                        out=bank[:, c0 : c0 + P], in_=words[:, 256 * g + e : 256 * (g + 1) : 2], identity=ident[:]
+                    )
+            return bank
+
+        def a_square(i, bank):
+            grp = keep.tile([P, 1024], BF16, name="k_grp%d" % i, tag="k_grp%d" % i, align_bytes=64)
+            nc.scalar.activation(
+                out=grp[:].rearrange("p (q e c) -> p q e c", e=2, c=2),
+                in_=bank[:].bitcast(BF16).rearrange("p (e q c) -> p q e c", e=2, c=2),
+                func=ACT.Square,
+            )
+            k_grp[i] = grp
+
+        def a_quant(i):
+            codes = keep.tile([P, 256], U32, name="k_codes%d" % i, tag="k_codes%d" % i, align_bytes=64)
+            scales = keep.tile([P, 256], U8, name="k_scales%d" % i, tag="k_scales%d" % i, align_bytes=64)
+            nc.vector.quantize_mx(out=codes[:].bitcast(FP8X4), scales=scales[:], in_=k_grp[i][:])
+            k_codes[i] = codes
+            k_scales[i] = scales
+
+        s_raw = []
+        for g in range(2):
+            s_raw_g = keep.tile([P, 4, OUTF], BF16, name="s_raw%d" % g, tag="s_raw%d" % g)
+            s_raw.append(s_raw_g)
+        for k in range(8):
+            u, s = divmod(k, 2)
+            g, t = divmod(k, 4)
+            bank = psum.tile([P, OUTF], BANK_DT, name="bank_s%d" % k, tag="bank")
+            nc.tensor.matmul_mx(
+                out=bank[:],
+                lhsT=x_codes[u][:, s * P : (s + 1) * P].bitcast(FP8X4),
+                lhsT_scale=x_scales[u][:, s * P : (s + 1) * P],
+                rhs=w_codes[:].bitcast(FP8X4),
+                rhs_scale=w_scales[:],
+                start=True,
+                stop=True,
+            )
+            if k in SC_ON_VECTOR:
+                nc.vector.tensor_copy(out=s_raw[g][:, t, :], in_=bank[:])
+            else:
+                nc.scalar.copy(out=s_raw[g][:, t, :], in_=bank[:])
+
+        banks_a = {}
+        for i in range(AHEAD):
+            a_square(i, a_turn(i))
+        banks_a[AHEAD] = a_turn(AHEAD)
+        bank_b = psum.tile([P, OUTF], F32, name="bank_b", tag="bank")
+        nc.tensor.matmul(out=bank_b[:], lhsT=ones[:], rhs=bias_row[:], start=True, stop=True)
+        b1 = keep.tile([P, OUTF], F32, name="b1", tag="b1")
+
+        s_codes = []
+        s_scales = []
+        for g in range(2):
+            grp = keep.tile([P, OUTF, 4], BF16, name="s_grp%d" % g, tag="s_grp%d" % g, align_bytes=64)
+            codes = keep.tile([P, OUTF], U32, name="s_codes%d" % g, tag="s_codes%d" % g, align_bytes=64)
+            scales = keep.tile([P, OUTF], U8, name="s_scales%d" % g, tag="s_scales%d" % g, align_bytes=64)
+            for c in range(2):
+                cols = slice(c * HALF, (c + 1) * HALF)
+                nc.vector.tensor_copy(out=grp[:, cols, :], in_=s_raw[g][:, :, cols].rearrange("p t o -> p o t"))
+            if g == 1:
+                a_quant(0)
+            for c in range(2):
+                cols = slice(c * HALF, (c + 1) * HALF)
+                nc.vector.quantize_mx(
+                    out=codes[:, cols].bitcast(FP8X4),
+                    scales=scales[:, cols],
+                    in_=grp[:, cols, :].rearrange("p o t -> p (o t)"),
+                )
+            s_codes.append(codes)
+            s_scales.append(scales)
+
+        accs = {}
+        vps = {}
+        negs = {}
+        exps = {}
+
+        def pieces(i):
+            if i in SPLIT_TILES:
+                return [slice(0, HALF), slice(HALF, OUTF)]
+            return [slice(0, OUTF)]
+
+        def multiply(i):
+            acc = psum.tile([P, OUTF], F32, name="acc%d" % i, tag="bank")
+            for g in range(2):
+                nc.tensor.matmul_mx(
+                    out=acc[:],
+                    lhsT=k_codes[i][:, g * P : (g + 1) * P].bitcast(FP8X4),
+                    lhsT_scale=k_scales[i][:, g * P : (g + 1) * P],
+                    rhs=s_codes[g][:].bitcast(FP8X4),
+                    rhs_scale=s_scales[g][:],
+                    start=(g == 0),
+                    stop=(g == 1),
+                )
+            accs[i] = acc
+
+        def add_bias(i):
+            vp = keep.tile([P, OUTF], F32, name="vp%d" % i, tag="vp%d" % i)
+            nc.vector.tensor_tensor(out=vp[:], in0=accs[i][:], in1=b1[:], op=ALU.add)
+            vps[i] = vp
+            neg = keep.tile([P, OUTF], F32, name="neg%d" % i, tag="neg%d" % i)
+            negs[i] = neg
+
+        def clamp_vector(i):
+            nc.vector.tensor_scalar(
+                out=negs[i][:], in0=vps[i][:], scalar1=-1.0, scalar2=1.0, op0=ALU.min, op1=ALU.add
+            )
+
+        def exponent(i):
+            on_scalar = i in MIN_ON_SCALAR
+            if on_scalar:
+                nc.scalar.activation(out=negs[i][:], in_=vps[i][:], func=ACT.Relu, scale=-1.0, bias=-1.0)
+            ex = keep.tile([P, OUTF], F32, name="ex%d" % i, tag="ex%d" % i)
+            for cols in pieces(i):
+                nc.scalar.activation(
+                    out=ex[:, cols], in_=negs[i][:, cols], func=ACT.Exp, scale=(-1.0 if on_scalar else 1.0)
+                )
+            exps[i] = ex
+
+        def finish(i):
+            res = keep.tile([P, OUTF], F32, name="res%d" % i, tag="res%d" % i)
+            for cols in pieces(i):
+                nc.vector.scalar_tensor_tensor(
+                    out=res[:, cols], in0=vps[i][:, cols], scalar=-1.0, in1=exps[i][:, cols], op0=ALU.max, op1=ALU.add
+                )
+                nc.sync.dma_start(out=out[i * P : (i + 1) * P, cols], in_=res[:, cols])
+
+        multiply(0)
+        a_quant(1)
+        nc.vector.tensor_scalar_add(out=b1[:], in0=bank_b[:], scalar1=-1.0)
+        add_bias(0)
+        a_quant(2)
+        clamp_vector(0)
+        for j in range(9):
+            if j + 1 < 8:
+                multiply(j + 1)
+            if j + AHEAD + 1 < 8:
+                banks_a[j + AHEAD + 1] = a_turn(j + AHEAD + 1)
+            if j + AHEAD < 8:
+                a_square(j + AHEAD, banks_a[j + AHEAD])
+            if j < 8:
+                exponent(j)
+            if AHEAD <= j + AHEAD - 1 < 8:
+                a_quant(j + AHEAD - 1)
+            if j + 1 < 8:
+                add_bias(j + 1)
+            if j >= 1:
+                finish(j - 1)
+            if j + 1 < 8 and (j + 1) not in MIN_ON_SCALAR:
+                clamp_vector(j + 1)

@@ -19,7 +19,9 @@ FEAT = 512
 OUTF = 512
 MANUAL = True
 AHEAD = 3
-NWARM = 6
+NWARM = 5
+NWARM_LATE = 3
+XC_ON_VECTOR = (1,)
 MIN_ON_SCALAR = (5, 6)
 SPLIT_TILES = (7,)
 SC_ON_VECTOR = (1, 3)
@@ -72,7 +74,10 @@ def tile_netgraphconvolution_kernel(tc, x, adj, weight, bias, out):
         HALF = OUTF // 2
         for c in range(2):
             cols = slice(c * HALF, (c + 1) * HALF)
-            nc.vector.tensor_copy(out=w_grp[:, cols, :], in_=w_raw[:, :, cols].rearrange("p j o -> p o j"))
+            nc.vector.tensor_copy(
+                out=w_grp[:, cols, :].rearrange("p (c i) j -> p c j i", i=4),
+                in_=w_raw[:, :, cols].rearrange("p j (c i) -> p c j i", i=4),
+            )
         for c in range(2):
             cols = slice(c * HALF, (c + 1) * HALF)
             nc.vector.quantize_mx(
@@ -93,7 +98,8 @@ def tile_netgraphconvolution_kernel(tc, x, adj, weight, bias, out):
                     c0 = e * 256 + s * P
                     nc.tensor.transpose(out=bank[:, c0 : c0 + P], in_=words[:, e:256:2], identity=ident[:])
             grp = keep.tile([P, 1024], BF16, name="x_grp%d" % u, tag="x_grp%d" % u, align_bytes=64)
-            nc.scalar.copy(
+            copy = nc.vector.tensor_copy if u in XC_ON_VECTOR else nc.scalar.copy
+            copy(
                 out=grp[:].bitcast(F32).rearrange("p (q e) -> p q e", e=2),
                 in_=bank[:].rearrange("p (e q) -> p q e", e=2),
             )
@@ -180,7 +186,20 @@ def tile_netgraphconvolution_kernel(tc, x, adj, weight, bias, out):
             scales = keep.tile([P, OUTF], U8, name="s_scales%d" % g, tag="s_scales%d" % g, align_bytes=64)
             for c in range(2):
                 cols = slice(c * HALF, (c + 1) * HALF)
-                nc.vector.tensor_copy(out=grp[:, cols, :], in_=s_raw[g][:, :, cols].rearrange("p t o -> p o t"))
+                nc.vector.tensor_copy(
+                    out=grp[:, cols, :].rearrange("p (c i) t -> p c t i", i=4),
+                    in_=s_raw[g][:, :, cols].rearrange("p t (c i) -> p c t i", i=4),
+                )
+                if g == 1 and c == 0:
+                    bank_w2 = psum.tile([P, OUTF], F32, name="bank_w2", tag="bank")
+                    for n in range(NWARM_LATE):
+                        nc.tensor.matmul(
+                            out=bank_w2[:],
+                            lhsT=ones[:],
+                            rhs=grp[:, 0:P, :].rearrange("p o t -> p (o t)"),
+                            start=True,
+                            stop=True,
+                        )
             if g == 1:
                 a_quant(0)
             for c in range(2):

@@ -17,15 +17,18 @@ P = 128
 NODES = 1024
 FEAT = 512
 OUTF = 512
-MANUAL = True
-AHEAD = 3
+HALF = OUTF // 2
+NT = NODES // P
 NWARM = 5
 NWARM_LATE = 3
-XC_ON_VECTOR = (1,)
-MIN_ON_SCALAR = (5, 6)
+XC_ON_VECTOR = (0,)
+SC_ON_VECTOR = ((0, 0), (1, 0))
+MIN_ON_SCALAR = (4, 5, 6)
 SPLIT_TILES = (7,)
-SC_ON_VECTOR = (1, 3)
-BANK_DT = BF16
+EARLY_TURNS = 2
+EARLY_SQUARES = 1
+WI_ON_SCALAR = ()
+AHEAD = 3
 
 
 def tile_netgraphconvolution_kernel(tc, x, adj, weight, bias, out):
@@ -33,22 +36,26 @@ def tile_netgraphconvolution_kernel(tc, x, adj, weight, bias, out):
     with ExitStack() as ctx:
         keep = ctx.enter_context(tc.tile_pool(name="keep", bufs=1))
         psum = ctx.enter_context(tc.psum_pool(name="psum", bufs=8))
-        if MANUAL:
-            ctx.enter_context(tc.manual_schedule())
+        ctx.enter_context(tc.manual_schedule())
 
         bias_row = keep.tile([P, OUTF], BF16, name="bias_row", tag="bias_row")
         ones = keep.tile([P, P], BF16, name="ones", tag="ones")
         warm = keep.tile([P, 8], F32, name="warm", tag="warm")
         zeros = keep.tile([P, OUTF], BF16, name="zeros", tag="zeros")
+        halves = [slice(0, HALF), slice(HALF, OUTF)]
+        nc.gpsimd.memset(bias_row[:], 0.0)
         nc.vector.memset(warm[:], 0.0)
         nc.vector.memset(ones[:], 1.0)
         nc.vector.memset(zeros[:], 0.0)
-        nc.vector.memset(bias_row[:], 0.0)
         nc.scalar.activation(out=warm[:, 4:8], in_=warm[:, 0:4], func=ACT.Exp)
-        nc.scalar.dma_start(out=bias_row[0:1, :], in_=bias.rearrange("(a o) -> a o", a=1))
+        nc.sync.dma_start(out=bias_row[0:1, :], in_=bias.rearrange("(a o) -> a o", a=1))
 
-        w_raw = keep.tile([P, 4, OUTF], BF16, name="w_raw", tag="w_raw")
-        nc.sync.dma_start(out=w_raw[:], in_=weight.rearrange("(p j) o -> p j o", j=4))
+        w_view = weight.rearrange("(p j) o -> p j o", j=4)
+        w_raw = []
+        for c in range(2):
+            t = keep.tile([P, 4, HALF], BF16, name="w_raw%d" % c, tag="w_raw%d" % c)
+            nc.sync.dma_start(out=t[:], in_=w_view[:, :, halves[c]])
+            w_raw.append(t)
         x_view = x.rearrange("(u m s) f -> u m s f", m=P, s=4)
         x_raw = []
         for u in range(4):
@@ -57,7 +64,7 @@ def tile_netgraphconvolution_kernel(tc, x, adj, weight, bias, out):
             nc.sync.dma_start(out=t[:], in_=x_view[g, :, 2 * h : 2 * h + 2, :])
             x_raw.append(t)
         a_raw = []
-        for i in range(8):
+        for i in range(NT):
             t = keep.tile([P, NODES], BF16, name="a_raw%d" % i, tag="a_raw%d" % i)
             nc.sync.dma_start(out=t[:], in_=adj[i * P : (i + 1) * P, :])
             a_raw.append(t)
@@ -67,28 +74,33 @@ def tile_netgraphconvolution_kernel(tc, x, adj, weight, bias, out):
         bank_w = psum.tile([P, OUTF], F32, name="bank_w", tag="bank")
         for n in range(NWARM):
             nc.tensor.matmul(out=bank_w[:], lhsT=ones[:], rhs=zeros[:], start=True, stop=True)
+        bank_b = psum.tile([P, OUTF], F32, name="bank_b", tag="bank")
+        nc.tensor.matmul(out=bank_b[:], lhsT=ones[:], rhs=bias_row[:], start=True, stop=True)
+        b1 = keep.tile([P, OUTF], F32, name="b1", tag="b1")
+        nc.scalar.activation(out=b1[:], in_=bank_b[:], func=ACT.Copy, bias=-1.0)
 
-        w_grp = keep.tile([P, OUTF, 4], BF16, name="w_grp", tag="w_grp", align_bytes=64)
         w_codes = keep.tile([P, OUTF], U32, name="w_codes", tag="w_codes", align_bytes=64)
         w_scales = keep.tile([P, OUTF], U8, name="w_scales", tag="w_scales", align_bytes=64)
-        HALF = OUTF // 2
+        w_grp = []
         for c in range(2):
-            cols = slice(c * HALF, (c + 1) * HALF)
-            nc.vector.tensor_copy(
-                out=w_grp[:, cols, :].rearrange("p (c i) j -> p c j i", i=4),
-                in_=w_raw[:, :, cols].rearrange("p j (c i) -> p c j i", i=4),
+            t = keep.tile([P, HALF, 4], BF16, name="w_grp%d" % c, tag="w_grp%d" % c, align_bytes=64)
+            copy = nc.scalar.copy if c in WI_ON_SCALAR else nc.vector.tensor_copy
+            copy(
+                out=t[:].rearrange("p (c i) j -> p c j i", i=4),
+                in_=w_raw[c][:].rearrange("p j (c i) -> p c j i", i=4),
             )
+            w_grp.append(t)
         for c in range(2):
-            cols = slice(c * HALF, (c + 1) * HALF)
             nc.vector.quantize_mx(
-                out=w_codes[:, cols].bitcast(FP8X4),
-                scales=w_scales[:, cols],
-                in_=w_grp[:, cols, :].rearrange("p o j -> p (o j)"),
+                out=w_codes[:, halves[c]].bitcast(FP8X4),
+                scales=w_scales[:, halves[c]],
+                in_=w_grp[c][:].rearrange("p o j -> p (o j)"),
             )
 
-        x_codes = []
-        x_scales = []
-        x_grp = []
+        x_bank = {}
+        x_grp = {}
+        x_codes = {}
+        x_scales = {}
 
         def x_turn(u):
             bank = psum.tile([P, 512], F32, name="bank_x%d" % u, tag="bank")
@@ -97,26 +109,25 @@ def tile_netgraphconvolution_kernel(tc, x, adj, weight, bias, out):
                 for e in range(2):
                     c0 = e * 256 + s * P
                     nc.tensor.transpose(out=bank[:, c0 : c0 + P], in_=words[:, e:256:2], identity=ident[:])
+            x_bank[u] = bank
+
+        def x_copy(u):
             grp = keep.tile([P, 1024], BF16, name="x_grp%d" % u, tag="x_grp%d" % u, align_bytes=64)
             copy = nc.vector.tensor_copy if u in XC_ON_VECTOR else nc.scalar.copy
             copy(
                 out=grp[:].bitcast(F32).rearrange("p (q e) -> p q e", e=2),
-                in_=bank[:].rearrange("p (e q) -> p q e", e=2),
+                in_=x_bank[u][:].rearrange("p (e q) -> p q e", e=2),
             )
-            x_grp.append(grp)
+            x_grp[u] = grp
 
         def x_quant(u):
             codes = keep.tile([P, 256], U32, name="x_codes%d" % u, tag="x_codes%d" % u, align_bytes=64)
             scales = keep.tile([P, 256], U8, name="x_scales%d" % u, tag="x_scales%d" % u, align_bytes=64)
             nc.vector.quantize_mx(out=codes[:].bitcast(FP8X4), scales=scales[:], in_=x_grp[u][:])
-            x_codes.append(codes)
-            x_scales.append(scales)
+            x_codes[u] = codes
+            x_scales[u] = scales
 
-        for u in range(4):
-            x_turn(u)
-            x_quant(u)
-
-
+        a_bank = {}
         k_grp = {}
         k_codes = {}
         k_scales = {}
@@ -130,13 +141,13 @@ def tile_netgraphconvolution_kernel(tc, x, adj, weight, bias, out):
                     nc.tensor.transpose(
                         out=bank[:, c0 : c0 + P], in_=words[:, 256 * g + e : 256 * (g + 1) : 2], identity=ident[:]
                     )
-            return bank
+            a_bank[i] = bank
 
-        def a_square(i, bank):
+        def a_square(i):
             grp = keep.tile([P, 1024], BF16, name="k_grp%d" % i, tag="k_grp%d" % i, align_bytes=64)
             nc.scalar.activation(
                 out=grp[:].rearrange("p (q e c) -> p q e c", e=2, c=2),
-                in_=bank[:].bitcast(BF16).rearrange("p (e q c) -> p q e c", e=2, c=2),
+                in_=a_bank[i][:].bitcast(BF16).rearrange("p (e q c) -> p q e c", e=2, c=2),
                 func=ACT.Square,
             )
             k_grp[i] = grp
@@ -148,69 +159,43 @@ def tile_netgraphconvolution_kernel(tc, x, adj, weight, bias, out):
             k_codes[i] = codes
             k_scales[i] = scales
 
-        s_raw = []
-        for g in range(2):
-            s_raw_g = keep.tile([P, 4, OUTF], BF16, name="s_raw%d" % g, tag="s_raw%d" % g)
-            s_raw.append(s_raw_g)
-        for k in range(8):
-            u, s = divmod(k, 2)
-            g, t = divmod(k, 4)
-            bank = psum.tile([P, OUTF], BANK_DT, name="bank_s%d" % k, tag="bank")
-            nc.tensor.matmul_mx(
-                out=bank[:],
-                lhsT=x_codes[u][:, s * P : (s + 1) * P].bitcast(FP8X4),
-                lhsT_scale=x_scales[u][:, s * P : (s + 1) * P],
-                rhs=w_codes[:].bitcast(FP8X4),
-                rhs_scale=w_scales[:],
-                start=True,
-                stop=True,
-            )
-            if k in SC_ON_VECTOR:
-                nc.vector.tensor_copy(out=s_raw[g][:, t, :], in_=bank[:])
-            else:
-                nc.scalar.copy(out=s_raw[g][:, t, :], in_=bank[:])
-
-        banks_a = {}
-        for i in range(AHEAD):
-            a_square(i, a_turn(i))
-        banks_a[AHEAD] = a_turn(AHEAD)
-        bank_b = psum.tile([P, OUTF], F32, name="bank_b", tag="bank")
-        nc.tensor.matmul(out=bank_b[:], lhsT=ones[:], rhs=bias_row[:], start=True, stop=True)
-        b1 = keep.tile([P, OUTF], F32, name="b1", tag="b1")
-
+        s_bank = {}
+        s_grp = []
         s_codes = []
         s_scales = []
         for g in range(2):
-            grp = keep.tile([P, OUTF, 4], BF16, name="s_grp%d" % g, tag="s_grp%d" % g, align_bytes=64)
-            codes = keep.tile([P, OUTF], U32, name="s_codes%d" % g, tag="s_codes%d" % g, align_bytes=64)
-            scales = keep.tile([P, OUTF], U8, name="s_scales%d" % g, tag="s_scales%d" % g, align_bytes=64)
-            for c in range(2):
-                cols = slice(c * HALF, (c + 1) * HALF)
-                nc.vector.tensor_copy(
-                    out=grp[:, cols, :].rearrange("p (c i) t -> p c t i", i=4),
-                    in_=s_raw[g][:, :, cols].rearrange("p t (c i) -> p c t i", i=4),
+            s_grp_g = keep.tile([P, OUTF, 4], BF16, name="s_grp%d" % g, tag="s_grp%d" % g, align_bytes=64)
+            s_codes_g = keep.tile([P, OUTF], U32, name="s_codes%d" % g, tag="s_codes%d" % g, align_bytes=64)
+            s_scales_g = keep.tile([P, OUTF], U8, name="s_scales%d" % g, tag="s_scales%d" % g, align_bytes=64)
+            s_grp.append(s_grp_g)
+            s_codes.append(s_codes_g)
+            s_scales.append(s_scales_g)
+
+        def s_multiply(g, c):
+            bank = psum.tile([P, 4, HALF], BF16, name="bank_s%d%d" % (g, c), tag="bank")
+            for t in range(4):
+                u, s = divmod(4 * g + t, 2)
+                nc.tensor.matmul_mx(
+                    out=bank[:, t, :],
+                    lhsT=x_codes[u][:, s * P : (s + 1) * P].bitcast(FP8X4),
+                    lhsT_scale=x_scales[u][:, s * P : (s + 1) * P],
+                    rhs=w_codes[:, halves[c]].bitcast(FP8X4),
+                    rhs_scale=w_scales[:, halves[c]],
+                    start=True,
+                    stop=True,
                 )
-                if g == 1 and c == 0:
-                    bank_w2 = psum.tile([P, OUTF], F32, name="bank_w2", tag="bank")
-                    for n in range(NWARM_LATE):
-                        nc.tensor.matmul(
-                            out=bank_w2[:],
-                            lhsT=ones[:],
-                            rhs=grp[:, 0:P, :].rearrange("p o t -> p (o t)"),
-                            start=True,
-                            stop=True,
-                        )
-            if g == 1:
-                a_quant(0)
-            for c in range(2):
-                cols = slice(c * HALF, (c + 1) * HALF)
-                nc.vector.quantize_mx(
-                    out=codes[:, cols].bitcast(FP8X4),
-                    scales=scales[:, cols],
-                    in_=grp[:, cols, :].rearrange("p o t -> p (o t)"),
-                )
-            s_codes.append(codes)
-            s_scales.append(scales)
+            s_bank[(g, c)] = bank
+
+        def s_copy(g, c):
+            copy = nc.vector.tensor_copy if (g, c) in SC_ON_VECTOR else nc.scalar.copy
+            copy(out=s_grp[g][:, halves[c], :], in_=s_bank[(g, c)][:].rearrange("p t o -> p o t"))
+
+        def s_quant(g, c):
+            nc.vector.quantize_mx(
+                out=s_codes[g][:, halves[c]].bitcast(FP8X4),
+                scales=s_scales[g][:, halves[c]],
+                in_=s_grp[g][:, halves[c], :].rearrange("p o t -> p (o t)"),
+            )
 
         accs = {}
         vps = {}
@@ -219,7 +204,7 @@ def tile_netgraphconvolution_kernel(tc, x, adj, weight, bias, out):
 
         def pieces(i):
             if i in SPLIT_TILES:
-                return [slice(0, HALF), slice(HALF, OUTF)]
+                return halves
             return [slice(0, OUTF)]
 
         def multiply(i):
@@ -267,26 +252,56 @@ def tile_netgraphconvolution_kernel(tc, x, adj, weight, bias, out):
                 )
                 nc.sync.dma_start(out=out[i * P : (i + 1) * P, cols], in_=res[:, cols])
 
+        for u in range(4):
+            x_turn(u)
+        for u in range(4):
+            x_copy(u)
+            x_quant(u)
+        a_turn(0)
+        a_square(0)
+        s_multiply(0, 0)
+        s_multiply(0, 1)
+        s_multiply(1, 0)
+        s_multiply(1, 1)
+        a_turn(1)
+        for g in range(2):
+            for c in range(2):
+                s_copy(g, c)
+        for i in range(EARLY_TURNS, AHEAD + 1):
+            a_turn(i)
+        bank_w2 = psum.tile([P, OUTF], F32, name="bank_w2", tag="bank")
+        for n in range(NWARM_LATE):
+            nc.tensor.matmul(
+                out=bank_w2[:], lhsT=ones[:], rhs=s_grp[1][:, 0:P, :].rearrange("p o t -> p (o t)"), start=True, stop=True
+            )
+        for i in range(EARLY_SQUARES, AHEAD):
+            a_square(i)
+        s_quant(0, 0)
+        s_quant(0, 1)
+        a_quant(0)
+        s_quant(1, 0)
+        s_quant(1, 1)
+
         multiply(0)
         a_quant(1)
-        nc.vector.tensor_scalar_add(out=b1[:], in0=bank_b[:], scalar1=-1.0)
         add_bias(0)
         a_quant(2)
-        clamp_vector(0)
-        for j in range(9):
-            if j + 1 < 8:
+        if 0 not in MIN_ON_SCALAR:
+            clamp_vector(0)
+        for j in range(NT + 1):
+            if j + 1 < NT:
                 multiply(j + 1)
-            if j + AHEAD + 1 < 8:
-                banks_a[j + AHEAD + 1] = a_turn(j + AHEAD + 1)
-            if j + AHEAD < 8:
-                a_square(j + AHEAD, banks_a[j + AHEAD])
-            if j < 8:
+            if j + AHEAD + 1 < NT:
+                a_turn(j + AHEAD + 1)
+            if j + AHEAD < NT:
+                a_square(j + AHEAD)
+            if j < NT:
                 exponent(j)
-            if AHEAD <= j + AHEAD - 1 < 8:
+            if AHEAD <= j + AHEAD - 1 < NT:
                 a_quant(j + AHEAD - 1)
-            if j + 1 < 8:
+            if j + 1 < NT:
                 add_bias(j + 1)
             if j >= 1:
                 finish(j - 1)
-            if j + 1 < 8 and (j + 1) not in MIN_ON_SCALAR:
+            if j + 1 < NT and (j + 1) not in MIN_ON_SCALAR:
                 clamp_vector(j + 1)

@@ -23,7 +23,7 @@ NWARM = 5
 NWARM_LATE = 3
 XC_ON_VECTOR = (0,)
 SC_ON_VECTOR = ((0, 0), (1, 0))
-MIN_ON_SCALAR = (4, 5, 6)
+MIN_ON_SCALAR = (5, 6)
 SPLIT_TILES = (7,)
 EARLY_TURNS = 2
 EARLY_SQUARES = 1
@@ -43,19 +43,15 @@ def tile_netgraphconvolution_kernel(tc, x, adj, weight, bias, out):
         warm = keep.tile([P, 8], F32, name="warm", tag="warm")
         zeros = keep.tile([P, OUTF], BF16, name="zeros", tag="zeros")
         halves = [slice(0, HALF), slice(HALF, OUTF)]
-        nc.gpsimd.memset(bias_row[:], 0.0)
+        nc.vector.memset(bias_row[:], 0.0)
         nc.vector.memset(warm[:], 0.0)
         nc.vector.memset(ones[:], 1.0)
         nc.vector.memset(zeros[:], 0.0)
         nc.scalar.activation(out=warm[:, 4:8], in_=warm[:, 0:4], func=ACT.Exp)
-        nc.sync.dma_start(out=bias_row[0:1, :], in_=bias.rearrange("(a o) -> a o", a=1))
 
-        w_view = weight.rearrange("(p j) o -> p j o", j=4)
-        w_raw = []
-        for c in range(2):
-            t = keep.tile([P, 4, HALF], BF16, name="w_raw%d" % c, tag="w_raw%d" % c)
-            nc.sync.dma_start(out=t[:], in_=w_view[:, :, halves[c]])
-            w_raw.append(t)
+        w_raw = keep.tile([P, 4, OUTF], BF16, name="w_raw", tag="w_raw")
+        nc.sync.dma_start(out=w_raw[:], in_=weight.rearrange("(p j) o -> p j o", j=4))
+        nc.sync.dma_start(out=bias_row[0:1, :], in_=bias.rearrange("(a o) -> a o", a=1))
         x_view = x.rearrange("(u m s) f -> u m s f", m=P, s=4)
         x_raw = []
         for u in range(4):
@@ -87,10 +83,11 @@ def tile_netgraphconvolution_kernel(tc, x, adj, weight, bias, out):
             copy = nc.scalar.copy if c in WI_ON_SCALAR else nc.vector.tensor_copy
             copy(
                 out=t[:].rearrange("p (c i) j -> p c j i", i=4),
-                in_=w_raw[c][:].rearrange("p j (c i) -> p c j i", i=4),
+                in_=w_raw[:, :, halves[c]].rearrange("p j (c i) -> p c j i", i=4),
             )
             w_grp.append(t)
-        for c in range(2):
+
+        def w_quant(c):
             nc.vector.quantize_mx(
                 out=w_codes[:, halves[c]].bitcast(FP8X4),
                 scales=w_scales[:, halves[c]],
@@ -254,7 +251,11 @@ def tile_netgraphconvolution_kernel(tc, x, adj, weight, bias, out):
 
         for u in range(4):
             x_turn(u)
-        for u in range(4):
+        w_quant(0)
+        x_copy(0)
+        w_quant(1)
+        x_quant(0)
+        for u in range(1, 4):
             x_copy(u)
             x_quant(u)
         a_turn(0)

@@ -73,7 +73,7 @@ def tile_netgraphconvolution_kernel(tc, x, adj, weight, bias, out):
         bank_b = psum.tile([P, OUTF], F32, name="bank_b", tag="bank")
         nc.tensor.matmul(out=bank_b[:], lhsT=ones[:], rhs=bias_row[:], start=True, stop=True)
         b1 = keep.tile([P, OUTF], F32, name="b1", tag="b1")
-        nc.scalar.activation(out=b1[:], in_=bank_b[:], func=ACT.Copy, bias=-1.0)
+        nc.scalar.copy(out=b1[:], in_=bank_b[:])
 
         w_codes = keep.tile([P, OUTF], U32, name="w_codes", tag="w_codes", align_bytes=64)
         w_scales = keep.tile([P, OUTF], U8, name="w_scales", tag="w_scales", align_bytes=64)
@@ -227,26 +227,28 @@ def tile_netgraphconvolution_kernel(tc, x, adj, weight, bias, out):
 
         def clamp_vector(i):
             nc.vector.tensor_scalar(
-                out=negs[i][:], in0=vps[i][:], scalar1=-1.0, scalar2=1.0, op0=ALU.min, op1=ALU.add
+                out=negs[i][:], in0=vps[i][:], scalar1=0.0, scalar2=-1.0, op0=ALU.max, op1=ALU.add
             )
 
         def exponent(i):
-            on_scalar = i in MIN_ON_SCALAR
-            if on_scalar:
-                nc.scalar.activation(out=negs[i][:], in_=vps[i][:], func=ACT.Relu, scale=-1.0, bias=-1.0)
             ex = keep.tile([P, OUTF], F32, name="ex%d" % i, tag="ex%d" % i)
             for cols in pieces(i):
-                nc.scalar.activation(
-                    out=ex[:, cols], in_=negs[i][:, cols], func=ACT.Exp, scale=(-1.0 if on_scalar else 1.0)
-                )
+                nc.scalar.activation(out=ex[:, cols], in_=vps[i][:, cols], func=ACT.Exp)
+            if i in MIN_ON_SCALAR:
+                nc.scalar.activation(out=negs[i][:], in_=vps[i][:], func=ACT.Relu)
             exps[i] = ex
 
         def finish(i):
             res = keep.tile([P, OUTF], F32, name="res%d" % i, tag="res%d" % i)
             for cols in pieces(i):
-                nc.vector.scalar_tensor_tensor(
-                    out=res[:, cols], in0=vps[i][:, cols], scalar=-1.0, in1=exps[i][:, cols], op0=ALU.max, op1=ALU.add
-                )
+                if i in MIN_ON_SCALAR:
+                    nc.vector.scalar_tensor_tensor(
+                        out=res[:, cols], in0=exps[i][:, cols], scalar=-1.0, in1=negs[i][:, cols], op0=ALU.add, op1=ALU.min
+                    )
+                else:
+                    nc.vector.scalar_tensor_tensor(
+                        out=res[:, cols], in0=exps[i][:, cols], scalar=1.0, in1=negs[i][:, cols], op0=ALU.min, op1=ALU.add
+                    )
                 nc.sync.dma_start(out=out[i * P : (i + 1) * P, cols], in_=res[:, cols])
 
         for u in range(4):

@@ -20,7 +20,6 @@ OUTF = 512
 HALF = OUTF // 2
 NT = NODES // P
 NWARM = 5
-NWARM_LATE = 3
 XC_ON_VECTOR = (0,)
 SC_ON_VECTOR = ((0, 0), (1, 0))
 MIN_ON_SCALAR = (5, 6)
@@ -131,6 +130,7 @@ def tile_netgraphconvolution_kernel(tc, x, adj, weight, bias, out):
 
         def a_turn(i):
             bank = psum.tile([P, 512], F32, name="bank_a%d" % i, tag="bank")
+            nc.tensor.matmul(out=bank[:, 0:P], lhsT=ident[:], rhs=ident[:], start=True, stop=True)
             words = a_raw[i][:].bitcast(F32)
             for g in range(2):
                 for e in range(2):
@@ -272,11 +272,6 @@ def tile_netgraphconvolution_kernel(tc, x, adj, weight, bias, out):
                 s_copy(g, c)
         for i in range(EARLY_TURNS, AHEAD + 1):
             a_turn(i)
-        bank_w2 = psum.tile([P, OUTF], F32, name="bank_w2", tag="bank")
-        for n in range(NWARM_LATE):
-            nc.tensor.matmul(
-                out=bank_w2[:], lhsT=ones[:], rhs=s_grp[1][:, 0:P, :].rearrange("p o t -> p (o t)"), start=True, stop=True
-            )
         for i in range(EARLY_SQUARES, AHEAD):
             a_square(i)
         s_quant(0, 0)

@@ -35,17 +35,16 @@ def tile_netgraphconvolution_kernel(tc, x, adj, weight, bias, out):
     with ExitStack() as ctx:
         keep = ctx.enter_context(tc.tile_pool(name="keep", bufs=1))
         psum = ctx.enter_context(tc.psum_pool(name="psum", bufs=8))
-        ctx.enter_context(tc.manual_schedule())
 
         bias_row = keep.tile([P, OUTF], BF16, name="bias_row", tag="bias_row")
         ones = keep.tile([P, P], BF16, name="ones", tag="ones")
         warm = keep.tile([P, 8], F32, name="warm", tag="warm")
         zeros = keep.tile([P, OUTF], BF16, name="zeros", tag="zeros")
         halves = [slice(0, HALF), slice(HALF, OUTF)]
-        nc.vector.memset(bias_row[:], 0.0)
+        nc.vector.memset(bias_row[:].bitcast(F32), 0.0)
         nc.vector.memset(warm[:], 0.0)
         nc.vector.memset(ones[:], 1.0)
-        nc.vector.memset(zeros[:], 0.0)
+        nc.vector.memset(zeros[:].bitcast(F32), 0.0)
         nc.scalar.activation(out=warm[:, 4:8], in_=warm[:, 0:4], func=ACT.Exp)
 
         w_raw = keep.tile([P, 4, OUTF], BF16, name="w_raw", tag="w_raw")

@@ -250,8 +250,13 @@ def tile_netgraphconvolution_kernel(tc, x, adj, weight, bias, out):
                     )
                 nc.sync.dma_start(out=out[i * P : (i + 1) * P, cols], in_=res[:, cols])
 
-        for u in range(4):
-            x_turn(u)
+        x_turn(0)
+        x_turn(1)
+        nc.tensor.matmul(
+            out=bank_w[:, 0:P], lhsT=ident[:], rhs=x_raw[1][:, 1, :].bitcast(F32)[:, 0:P], start=True, stop=True
+        )
+        x_turn(2)
+        x_turn(3)
         w_quant(0)
         x_copy(0)
         w_quant(1)

@@ -28,6 +28,7 @@ EARLY_TURNS = 2
 EARLY_SQUARES = 1
 WI_ON_SCALAR = ()
 AHEAD = 3
+FILL_TILES = (0, 2)
 
 
 def tile_netgraphconvolution_kernel(tc, x, adj, weight, bias, out):
@@ -129,7 +130,8 @@ def tile_netgraphconvolution_kernel(tc, x, adj, weight, bias, out):
 
         def a_turn(i):
             bank = psum.tile([P, 512], F32, name="bank_a%d" % i, tag="bank")
-            nc.tensor.matmul(out=bank[:, 0:P], lhsT=ident[:], rhs=ident[:], start=True, stop=True)
+            if i in FILL_TILES:
+                nc.tensor.matmul(out=bank[:, 0:P], lhsT=ident[:], rhs=ident[:], start=True, stop=True)
             words = a_raw[i][:].bitcast(F32)
             for g in range(2):
                 for e in range(2):

@@ -28,7 +28,7 @@ EARLY_TURNS = 2
 EARLY_SQUARES = 1
 WI_ON_SCALAR = ()
 AHEAD = 3
-FILL_TILES = (0, 2)
+FILL_TILES = (2,)
 
 
 def tile_netgraphconvolution_kernel(tc, x, adj, weight, bias, out):

@@ -61,7 +61,12 @@ def tile_netgraphconvolution_kernel(tc, x, adj, weight, bias, out):
         a_raw = []
         for i in range(NT):
             t = keep.tile([P, NODES], BF16, name="a_raw%d" % i, tag="a_raw%d" % i)
-            nc.sync.dma_start(out=t[:], in_=adj[i * P : (i + 1) * P, :])
+            if i == 0:
+                for g in range(2):
+                    k_cols = slice(g * 512, (g + 1) * 512)
+                    nc.sync.dma_start(out=t[:, k_cols], in_=adj[i * P : (i + 1) * P, k_cols])
+            else:
+                nc.sync.dma_start(out=t[:], in_=adj[i * P : (i + 1) * P, :])
             a_raw.append(t)
 
         ident = keep.tile([P, P], F32, name="ident", tag="ident")

@@ -21,7 +21,7 @@ HALF = OUTF // 2
 NT = NODES // P
 NWARM = 5
 XC_ON_VECTOR = (0,)
-SC_ON_VECTOR = ((0, 0), (1, 0))
+SC_ON_VECTOR = ((0, 0), (1, 1))
 MIN_ON_SCALAR = (5, 6)
 SPLIT_TILES = (7,)
 EARLY_TURNS = 2

@@ -20,7 +20,7 @@ OUTF = 512
 HALF = OUTF // 2
 NT = NODES // P
 NWARM = 5
-XC_ON_VECTOR = (0,)
+XC_ON_VECTOR = (0, 3)
 SC_ON_VECTOR = ((0, 0), (1, 1))
 MIN_ON_SCALAR = (5, 6)
 SPLIT_TILES = (7,)
@@ -29,6 +29,7 @@ EARLY_SQUARES = 1
 WI_ON_SCALAR = ()
 AHEAD = 3
 FILL_TILES = (2,)
+TWO_BANK_TILES = (0,)
 
 
 def tile_netgraphconvolution_kernel(tc, x, adj, weight, bias, out):
@@ -134,6 +135,17 @@ def tile_netgraphconvolution_kernel(tc, x, adj, weight, bias, out):
         k_scales = {}
 
         def a_turn(i):
+            if i in TWO_BANK_TILES:
+                words = a_raw[i][:].bitcast(F32)
+                a_bank[i] = []
+                for g in range(2):
+                    half = psum.tile([P, 256], F32, name="bank_a%d_%d" % (i, g), tag="bank")
+                    for e in range(2):
+                        nc.tensor.transpose(
+                            out=half[:, e * P : (e + 1) * P], in_=words[:, 256 * g + e : 256 * (g + 1) : 2], identity=ident[:]
+                        )
+                    a_bank[i].append(half)
+                return
             bank = psum.tile([P, 512], F32, name="bank_a%d" % i, tag="bank")
             if i in FILL_TILES:
                 nc.tensor.matmul(out=bank[:, 0:P], lhsT=ident[:], rhs=ident[:], start=True, stop=True)
@@ -148,6 +160,15 @@ def tile_netgraphconvolution_kernel(tc, x, adj, weight, bias, out):
 
         def a_square(i):
             grp = keep.tile([P, 1024], BF16, name="k_grp%d" % i, tag="k_grp%d" % i, align_bytes=64)
+            k_grp[i] = grp
+            if i in TWO_BANK_TILES:
+                for g in range(2):
+                    nc.scalar.activation(
+                        out=grp[:, g * 512 : (g + 1) * 512].rearrange("p (q e c) -> p q e c", e=2, c=2),
+                        in_=a_bank[i][g][:].bitcast(BF16).rearrange("p (e q c) -> p q e c", e=2, c=2),
+                        func=ACT.Square,
+                    )
+                return
             nc.scalar.activation(
                 out=grp[:].rearrange("p (q e c) -> p q e c", e=2, c=2),
                 in_=a_bank[i][:].bitcast(BF16).rearrange("p (e q c) -> p q e c", e=2, c=2),

@@ -30,6 +30,7 @@ WI_ON_SCALAR = ()
 AHEAD = 3
 FILL_TILES = (2,)
 TWO_BANK_TILES = (0,)
+TWO_BANK_UNITS = (3,)
 
 
 def tile_netgraphconvolution_kernel(tc, x, adj, weight, bias, out):
@@ -105,6 +106,15 @@ def tile_netgraphconvolution_kernel(tc, x, adj, weight, bias, out):
         x_scales = {}
 
         def x_turn(u):
+            if u in TWO_BANK_UNITS:
+                x_bank[u] = []
+                for s in range(2):
+                    words = x_raw[u][:, s, :].bitcast(F32)
+                    half = psum.tile([P, 256], F32, name="bank_x%d_%d" % (u, s), tag="bank")
+                    for e in range(2):
+                        nc.tensor.transpose(out=half[:, e * P : (e + 1) * P], in_=words[:, e:256:2], identity=ident[:])
+                    x_bank[u].append(half)
+                return
             bank = psum.tile([P, 512], F32, name="bank_x%d" % u, tag="bank")
             for s in range(2):
                 words = x_raw[u][:, s, :].bitcast(F32)
@@ -116,6 +126,14 @@ def tile_netgraphconvolution_kernel(tc, x, adj, weight, bias, out):
         def x_copy(u):
             grp = keep.tile([P, 1024], BF16, name="x_grp%d" % u, tag="x_grp%d" % u, align_bytes=64)
             copy = nc.vector.tensor_copy if u in XC_ON_VECTOR else nc.scalar.copy
+            x_grp[u] = grp
+            if u in TWO_BANK_UNITS:
+                for s in range(2):
+                    copy(
+                        out=grp[:, s * 512 : (s + 1) * 512].bitcast(F32).rearrange("p (q e) -> p q e", e=2),
+                        in_=x_bank[u][s][:].rearrange("p (e q) -> p q e", e=2),
+                    )
+                return
             copy(
                 out=grp[:].bitcast(F32).rearrange("p (q e) -> p q e", e=2),
                 in_=x_bank[u][:].rearrange("p (e q) -> p q e", e=2),
@@ -125,7 +143,15 @@ def tile_netgraphconvolution_kernel(tc, x, adj, weight, bias, out):
         def x_quant(u):
             codes = keep.tile([P, 256], U32, name="x_codes%d" % u, tag="x_codes%d" % u, align_bytes=64)
             scales = keep.tile([P, 256], U8, name="x_scales%d" % u, tag="x_scales%d" % u, align_bytes=64)
-            nc.vector.quantize_mx(out=codes[:].bitcast(FP8X4), scales=scales[:], in_=x_grp[u][:])
+            if u in TWO_BANK_UNITS:
+                for s in range(2):
+                    nc.vector.quantize_mx(
+                        out=codes[:, s * P : (s + 1) * P].bitcast(FP8X4),
+                        scales=scales[:, s * P : (s + 1) * P],
+                        in_=x_grp[u][:, s * 512 : (s + 1) * 512],
+                    )
+            else:
+                nc.vector.quantize_mx(out=codes[:].bitcast(FP8X4), scales=scales[:], in_=x_grp[u][:])
             x_codes[u] = codes
             x_scales[u] = scales
 

@@ -221,6 +221,26 @@ def tile_netgraphconvolution_kernel(tc, x, adj, weight, bias, out):
             s_codes.append(s_codes_g)
             s_scales.append(s_scales_g)
 
+        def s_multiply_narrow(q):
+            cols = slice(HALF + q * P, HALF + (q + 1) * P)
+            bank = psum.tile([P, 4, P], BF16, name="bank_s01_%d" % q, tag="bank")
+            for t in range(4):
+                u, s = divmod(t, 2)
+                nc.tensor.matmul_mx(
+                    out=bank[:, t, :],
+                    lhsT=x_codes[u][:, s * P : (s + 1) * P].bitcast(FP8X4),
+                    lhsT_scale=x_scales[u][:, s * P : (s + 1) * P],
+                    rhs=w_codes[:, cols].bitcast(FP8X4),
+                    rhs_scale=w_scales[:, cols],
+                    start=True,
+                    stop=True,
+                )
+            s_bank[(0, 1, q)] = bank
+
+        def s_copy_narrow(q):
+            cols = slice(HALF + q * P, HALF + (q + 1) * P)
+            nc.scalar.copy(out=s_grp[0][:, cols, :], in_=s_bank[(0, 1, q)][:].rearrange("p t o -> p o t"))
+
         def s_multiply(g, c):
             bank = psum.tile([P, 4, HALF], BF16, name="bank_s%d%d" % (g, c), tag="bank")
             for t in range(4):
@@ -321,13 +341,16 @@ def tile_netgraphconvolution_kernel(tc, x, adj, weight, bias, out):
         a_turn(0)
         a_square(0)
         s_multiply(0, 0)
-        s_multiply(0, 1)
+        s_multiply_narrow(0)
+        s_multiply_narrow(1)
         s_multiply(1, 0)
         s_multiply(1, 1)
         a_turn(1)
-        for g in range(2):
-            for c in range(2):
-                s_copy(g, c)
+        s_copy(0, 0)
+        s_copy_narrow(0)
+        s_copy_narrow(1)
+        s_copy(1, 0)
+        s_copy(1, 1)
         for i in range(EARLY_TURNS, AHEAD + 1):
             a_turn(i)
         for i in range(EARLY_SQUARES, AHEAD):

@@ -31,6 +31,7 @@ AHEAD = 3
 FILL_TILES = (2,)
 TWO_BANK_TILES = (0,)
 TWO_BANK_UNITS = (3,)
+HALVED_FIRST = (0,)
 
 
 def tile_netgraphconvolution_kernel(tc, x, adj, weight, bias, out):
@@ -45,10 +46,9 @@ def tile_netgraphconvolution_kernel(tc, x, adj, weight, bias, out):
         zeros = keep.tile([P, OUTF], BF16, name="zeros", tag="zeros")
         halves = [slice(0, HALF), slice(HALF, OUTF)]
         nc.vector.memset(bias_row[:].bitcast(F32), 0.0)
-        nc.vector.memset(warm[:], 0.0)
         nc.vector.memset(ones[:], 1.0)
         nc.vector.memset(zeros[:].bitcast(F32), 0.0)
-        nc.scalar.activation(out=warm[:, 4:8], in_=warm[:, 0:4], func=ACT.Exp)
+        nc.scalar.activation(out=warm[:, 4:8], in_=zeros[:, 0:4], func=ACT.Exp)
 
         w_raw = keep.tile([P, 4, OUTF], BF16, name="w_raw", tag="w_raw")
         nc.sync.dma_start(out=w_raw[:], in_=weight.rearrange("(p j) o -> p j o", j=4))
@@ -291,9 +291,27 @@ def tile_netgraphconvolution_kernel(tc, x, adj, weight, bias, out):
                 )
             accs[i] = acc
 
+        def multiply_half(i, c):
+            acc = psum.tile([P, HALF], F32, name="acc%d_%d" % (i, c), tag="bank")
+            for g in range(2):
+                nc.tensor.matmul_mx(
+                    out=acc[:],
+                    lhsT=k_codes[i][:, g * P : (g + 1) * P].bitcast(FP8X4),
+                    lhsT_scale=k_scales[i][:, g * P : (g + 1) * P],
+                    rhs=s_codes[g][:, halves[c]].bitcast(FP8X4),
+                    rhs_scale=s_scales[g][:, halves[c]],
+                    start=(g == 0),
+                    stop=(g == 1),
+                )
+            accs[(i, c)] = acc
+
         def add_bias(i):
             vp = keep.tile([P, OUTF], F32, name="vp%d" % i, tag="vp%d" % i)
-            nc.vector.tensor_tensor(out=vp[:], in0=accs[i][:], in1=b1[:], op=ALU.add)
+            if i in HALVED_FIRST:
+                for c in range(2):
+                    nc.vector.tensor_tensor(out=vp[:, halves[c]], in0=accs[(i, c)][:], in1=b1[:, halves[c]], op=ALU.add)
+            else:
+                nc.vector.tensor_tensor(out=vp[:], in0=accs[i][:], in1=b1[:], op=ALU.add)
             vps[i] = vp
             neg = keep.tile([P, OUTF], F32, name="neg%d" % i, tag="neg%d" % i)
             negs[i] = neg
@@ -356,12 +374,13 @@ def tile_netgraphconvolution_kernel(tc, x, adj, weight, bias, out):
         for i in range(EARLY_SQUARES, AHEAD):
             a_square(i)
         s_quant(0, 0)
-        s_quant(0, 1)
         a_quant(0)
         s_quant(1, 0)
+        multiply_half(0, 0)
+        s_quant(0, 1)
         s_quant(1, 1)
 
-        multiply(0)
+        multiply_half(0, 1)
         a_quant(1)
         add_bias(0)
         a_quant(2)

@@ -31,7 +31,7 @@ AHEAD = 3
 FILL_TILES = (2,)
 TWO_BANK_TILES = (0,)
 TWO_BANK_UNITS = (3,)
-HALVED_FIRST = (0,)
+HALVED_FIRST = (0, 7)
 
 
 def tile_netgraphconvolution_kernel(tc, x, adj, weight, bias, out):
@@ -46,7 +46,7 @@ def tile_netgraphconvolution_kernel(tc, x, adj, weight, bias, out):
         zeros = keep.tile([P, OUTF], BF16, name="zeros", tag="zeros")
         halves = [slice(0, HALF), slice(HALF, OUTF)]
         nc.vector.memset(bias_row[:].bitcast(F32), 0.0)
-        nc.vector.memset(ones[:], 1.0)
+        nc.gpsimd.memset(ones[:], 1.0)
         nc.vector.memset(zeros[:].bitcast(F32), 0.0)
         nc.scalar.activation(out=warm[:, 4:8], in_=zeros[:, 0:4], func=ACT.Exp)
 
@@ -387,7 +387,10 @@ def tile_netgraphconvolution_kernel(tc, x, adj, weight, bias, out):
         if 0 not in MIN_ON_SCALAR:
             clamp_vector(0)
         for j in range(NT + 1):
-            if j + 1 < NT:
+            if j + 1 in HALVED_FIRST:
+                multiply_half(j + 1, 0)
+                multiply_half(j + 1, 1)
+            elif j + 1 < NT:
                 multiply(j + 1)
             if j + AHEAD + 1 < NT:
                 a_turn(j + AHEAD + 1)

@@ -392,8 +392,9 @@ def tile_netgraphconvolution_kernel(tc, x, adj, weight, bias, out):
                 multiply_half(j + 1, 1)
             elif j + 1 < NT:
                 multiply(j + 1)
-            if j + AHEAD + 1 < NT:
+            if j % 2 == 0 and j + AHEAD + 1 < NT:
                 a_turn(j + AHEAD + 1)
+                a_turn(j + AHEAD + 2)
             if j + AHEAD < NT:
                 a_square(j + AHEAD)
             if j < NT:

from contextlib import ExitStack

import concourse.mybir as mybir
from concourse.masks import make_identity

FLOPS = 2 * 1024 * 512 * 512 + 2 * 1024 * 1024 * 512

F32 = mybir.dt.float32
BF16 = mybir.dt.bfloat16
U32 = mybir.dt.uint32
U8 = mybir.dt.uint8
FP8X4 = mybir.dt.float8_e4m3fn_x4
ALU = mybir.AluOpType
ACT = mybir.ActivationFunctionType

P = 128
NODES = 1024
FEAT = 512
OUTF = 512
HALF = OUTF // 2
NT = NODES // P
NWARM = 5
XC_ON_VECTOR = (0, 3)
SC_ON_VECTOR = ((0, 0), (1, 1))
MIN_ON_SCALAR = (5, 6)
SPLIT_TILES = (7,)
EARLY_TURNS = 2
EARLY_SQUARES = 1
WI_ON_SCALAR = ()
AHEAD = 3
FILL_TILES = (2,)
TWO_BANK_TILES = (0,)
TWO_BANK_UNITS = (3,)
HALVED_FIRST = (0, 7)


def tile_netgraphconvolution_kernel(tc, x, adj, weight, bias, out):
    nc = tc.nc
    with ExitStack() as ctx:
        keep = ctx.enter_context(tc.tile_pool(name="keep", bufs=1))
        psum = ctx.enter_context(tc.psum_pool(name="psum", bufs=8))

        bias_row = keep.tile([P, OUTF], BF16, name="bias_row", tag="bias_row")
        ones = keep.tile([P, P], BF16, name="ones", tag="ones")
        warm = keep.tile([P, 8], F32, name="warm", tag="warm")
        zeros = keep.tile([P, OUTF], BF16, name="zeros", tag="zeros")
        halves = [slice(0, HALF), slice(HALF, OUTF)]
        nc.vector.memset(bias_row[:].bitcast(F32), 0.0)
        nc.gpsimd.memset(ones[:], 1.0)
        nc.vector.memset(zeros[:].bitcast(F32), 0.0)
        nc.scalar.activation(out=warm[:, 4:8], in_=zeros[:, 0:4], func=ACT.Exp)

        w_raw = keep.tile([P, 4, OUTF], BF16, name="w_raw", tag="w_raw")
        nc.sync.dma_start(out=w_raw[:], in_=weight.rearrange("(p j) o -> p j o", j=4))
        nc.sync.dma_start(out=bias_row[0:1, :], in_=bias.rearrange("(a o) -> a o", a=1))
        x_view = x.rearrange("(u m s) f -> u m s f", m=P, s=4)
        x_raw = []
        for u in range(4):
            t = keep.tile([P, 2, FEAT], BF16, name="x_raw%d" % u, tag="x_raw%d" % u)
            g, h = divmod(u, 2)
            nc.sync.dma_start(out=t[:], in_=x_view[g, :, 2 * h : 2 * h + 2, :])
            x_raw.append(t)
        a_raw = []
        for i in range(NT):
            t = keep.tile([P, NODES], BF16, name="a_raw%d" % i, tag="a_raw%d" % i)
            if i == 0:
                for g in range(2):
                    k_cols = slice(g * 512, (g + 1) * 512)
                    nc.sync.dma_start(out=t[:, k_cols], in_=adj[i * P : (i + 1) * P, k_cols])
            else:
                nc.sync.dma_start(out=t[:], in_=adj[i * P : (i + 1) * P, :])
            a_raw.append(t)

        ident = keep.tile([P, P], F32, name="ident", tag="ident")
        make_identity(nc, ident[:])
        bank_w = psum.tile([P, OUTF], F32, name="bank_w", tag="bank")
        for n in range(NWARM):
            nc.tensor.matmul(out=bank_w[:], lhsT=ones[:], rhs=zeros[:], start=True, stop=True)
        bank_b = psum.tile([P, OUTF], F32, name="bank_b", tag="bank")
        nc.tensor.matmul(out=bank_b[:], lhsT=ones[:], rhs=bias_row[:], start=True, stop=True)
        b1 = keep.tile([P, OUTF], F32, name="b1", tag="b1")
        nc.scalar.copy(out=b1[:], in_=bank_b[:])

        w_codes = keep.tile([P, OUTF], U32, name="w_codes", tag="w_codes", align_bytes=64)
        w_scales = keep.tile([P, OUTF], U8, name="w_scales", tag="w_scales", align_bytes=64)
        w_grp = []
        for c in range(2):
            t = keep.tile([P, HALF, 4], BF16, name="w_grp%d" % c, tag="w_grp%d" % c, align_bytes=64)
            copy = nc.scalar.copy if c in WI_ON_SCALAR else nc.vector.tensor_copy
            copy(
                out=t[:].rearrange("p (c i) j -> p c j i", i=4),
                in_=w_raw[:, :, halves[c]].rearrange("p j (c i) -> p c j i", i=4),
            )
            w_grp.append(t)

        def w_quant(c):
            nc.vector.quantize_mx(
                out=w_codes[:, halves[c]].bitcast(FP8X4),
                scales=w_scales[:, halves[c]],
                in_=w_grp[c][:].rearrange("p o j -> p (o j)"),
            )

        x_bank = {}
        x_grp = {}
        x_codes = {}
        x_scales = {}

        def x_turn(u):
            if u in TWO_BANK_UNITS:
                x_bank[u] = []
                for s in range(2):
                    words = x_raw[u][:, s, :].bitcast(F32)
                    half = psum.tile([P, 256], F32, name="bank_x%d_%d" % (u, s), tag="bank")
                    for e in range(2):
                        nc.tensor.transpose(out=half[:, e * P : (e + 1) * P], in_=words[:, e:256:2], identity=ident[:])
                    x_bank[u].append(half)
                return
            bank = psum.tile([P, 512], F32, name="bank_x%d" % u, tag="bank")
            for s in range(2):
                words = x_raw[u][:, s, :].bitcast(F32)
                for e in range(2):
                    c0 = e * 256 + s * P
                    nc.tensor.transpose(out=bank[:, c0 : c0 + P], in_=words[:, e:256:2], identity=ident[:])
            x_bank[u] = bank

        def x_copy(u):
            grp = keep.tile([P, 1024], BF16, name="x_grp%d" % u, tag="x_grp%d" % u, align_bytes=64)
            copy = nc.vector.tensor_copy if u in XC_ON_VECTOR else nc.scalar.copy
            x_grp[u] = grp
            if u in TWO_BANK_UNITS:
                for s in range(2):
                    copy(
                        out=grp[:, s * 512 : (s + 1) * 512].bitcast(F32).rearrange("p (q e) -> p q e", e=2),
                        in_=x_bank[u][s][:].rearrange("p (e q) -> p q e", e=2),
                    )
                return
            copy(
                out=grp[:].bitcast(F32).rearrange("p (q e) -> p q e", e=2),
                in_=x_bank[u][:].rearrange("p (e q) -> p q e", e=2),
            )
            x_grp[u] = grp

        def x_quant(u):
            codes = keep.tile([P, 256], U32, name="x_codes%d" % u, tag="x_codes%d" % u, align_bytes=64)
            scales = keep.tile([P, 256], U8, name="x_scales%d" % u, tag="x_scales%d" % u, align_bytes=64)
            if u in TWO_BANK_UNITS:
                for s in range(2):
                    nc.vector.quantize_mx(
                        out=codes[:, s * P : (s + 1) * P].bitcast(FP8X4),
                        scales=scales[:, s * P : (s + 1) * P],
                        in_=x_grp[u][:, s * 512 : (s + 1) * 512],
                    )
            else:
                nc.vector.quantize_mx(out=codes[:].bitcast(FP8X4), scales=scales[:], in_=x_grp[u][:])
            x_codes[u] = codes
            x_scales[u] = scales

        a_bank = {}
        k_grp = {}
        k_codes = {}
        k_scales = {}

        def a_turn(i):
            if i in TWO_BANK_TILES:
                words = a_raw[i][:].bitcast(F32)
                a_bank[i] = []
                for g in range(2):
                    half = psum.tile([P, 256], F32, name="bank_a%d_%d" % (i, g), tag="bank")
                    for e in range(2):
                        nc.tensor.transpose(
                            out=half[:, e * P : (e + 1) * P], in_=words[:, 256 * g + e : 256 * (g + 1) : 2], identity=ident[:]
                        )
                    a_bank[i].append(half)
                return
            bank = psum.tile([P, 512], F32, name="bank_a%d" % i, tag="bank")
            if i in FILL_TILES:
                nc.tensor.matmul(out=bank[:, 0:P], lhsT=ident[:], rhs=ident[:], start=True, stop=True)
            words = a_raw[i][:].bitcast(F32)
            for g in range(2):
                for e in range(2):
                    c0 = e * 256 + g * P
                    nc.tensor.transpose(
                        out=bank[:, c0 : c0 + P], in_=words[:, 256 * g + e : 256 * (g + 1) : 2], identity=ident[:]
                    )
            a_bank[i] = bank

        def a_square(i):
            grp = keep.tile([P, 1024], BF16, name="k_grp%d" % i, tag="k_grp%d" % i, align_bytes=64)
            k_grp[i] = grp
            if i in TWO_BANK_TILES:
                for g in range(2):
                    nc.scalar.activation(
                        out=grp[:, g * 512 : (g + 1) * 512].rearrange("p (q e c) -> p q e c", e=2, c=2),
                        in_=a_bank[i][g][:].bitcast(BF16).rearrange("p (e q c) -> p q e c", e=2, c=2),
                        func=ACT.Square,
                    )
                return
            nc.scalar.activation(
                out=grp[:].rearrange("p (q e c) -> p q e c", e=2, c=2),
                in_=a_bank[i][:].bitcast(BF16).rearrange("p (e q c) -> p q e c", e=2, c=2),
                func=ACT.Square,
            )
            k_grp[i] = grp

        def a_quant(i):
            codes = keep.tile([P, 256], U32, name="k_codes%d" % i, tag="k_codes%d" % i, align_bytes=64)
            scales = keep.tile([P, 256], U8, name="k_scales%d" % i, tag="k_scales%d" % i, align_bytes=64)
            nc.vector.quantize_mx(out=codes[:].bitcast(FP8X4), scales=scales[:], in_=k_grp[i][:])
            k_codes[i] = codes
            k_scales[i] = scales

        s_bank = {}
        s_grp = []
        s_codes = []
        s_scales = []
        for g in range(2):
            s_grp_g = keep.tile([P, OUTF, 4], BF16, name="s_grp%d" % g, tag="s_grp%d" % g, align_bytes=64)
            s_codes_g = keep.tile([P, OUTF], U32, name="s_codes%d" % g, tag="s_codes%d" % g, align_bytes=64)
            s_scales_g = keep.tile([P, OUTF], U8, name="s_scales%d" % g, tag="s_scales%d" % g, align_bytes=64)
            s_grp.append(s_grp_g)
            s_codes.append(s_codes_g)
            s_scales.append(s_scales_g)

        def s_multiply_narrow(q):
            cols = slice(HALF + q * P, HALF + (q + 1) * P)
            bank = psum.tile([P, 4, P], BF16, name="bank_s01_%d" % q, tag="bank")
            for t in range(4):
                u, s = divmod(t, 2)
                nc.tensor.matmul_mx(
                    out=bank[:, t, :],
                    lhsT=x_codes[u][:, s * P : (s + 1) * P].bitcast(FP8X4),
                    lhsT_scale=x_scales[u][:, s * P : (s + 1) * P],
                    rhs=w_codes[:, cols].bitcast(FP8X4),
                    rhs_scale=w_scales[:, cols],
                    start=True,
                    stop=True,
                )
            s_bank[(0, 1, q)] = bank

        def s_copy_narrow(q):
            cols = slice(HALF + q * P, HALF + (q + 1) * P)
            nc.scalar.copy(out=s_grp[0][:, cols, :], in_=s_bank[(0, 1, q)][:].rearrange("p t o -> p o t"))

        def s_multiply(g, c):
            bank = psum.tile([P, 4, HALF], BF16, name="bank_s%d%d" % (g, c), tag="bank")
            for t in range(4):
                u, s = divmod(4 * g + t, 2)
                nc.tensor.matmul_mx(
                    out=bank[:, t, :],
                    lhsT=x_codes[u][:, s * P : (s + 1) * P].bitcast(FP8X4),
                    lhsT_scale=x_scales[u][:, s * P : (s + 1) * P],
                    rhs=w_codes[:, halves[c]].bitcast(FP8X4),
                    rhs_scale=w_scales[:, halves[c]],
                    start=True,
                    stop=True,
                )
            s_bank[(g, c)] = bank

        def s_copy(g, c):
            copy = nc.vector.tensor_copy if (g, c) in SC_ON_VECTOR else nc.scalar.copy
            copy(out=s_grp[g][:, halves[c], :], in_=s_bank[(g, c)][:].rearrange("p t o -> p o t"))

        def s_quant(g, c):
            nc.vector.quantize_mx(
                out=s_codes[g][:, halves[c]].bitcast(FP8X4),
                scales=s_scales[g][:, halves[c]],
                in_=s_grp[g][:, halves[c], :].rearrange("p o t -> p (o t)"),
            )

        accs = {}
        vps = {}
        negs = {}
        exps = {}

        def pieces(i):
            if i in SPLIT_TILES:
                return halves
            return [slice(0, OUTF)]

        def multiply(i):
            acc = psum.tile([P, OUTF], F32, name="acc%d" % i, tag="bank")
            for g in range(2):
                nc.tensor.matmul_mx(
                    out=acc[:],
                    lhsT=k_codes[i][:, g * P : (g + 1) * P].bitcast(FP8X4),
                    lhsT_scale=k_scales[i][:, g * P : (g + 1) * P],
                    rhs=s_codes[g][:].bitcast(FP8X4),
                    rhs_scale=s_scales[g][:],
                    start=(g == 0),
                    stop=(g == 1),
                )
            accs[i] = acc

        def multiply_half(i, c):
            acc = psum.tile([P, HALF], F32, name="acc%d_%d" % (i, c), tag="bank")
            for g in range(2):
                nc.tensor.matmul_mx(
                    out=acc[:],
                    lhsT=k_codes[i][:, g * P : (g + 1) * P].bitcast(FP8X4),
                    lhsT_scale=k_scales[i][:, g * P : (g + 1) * P],
                    rhs=s_codes[g][:, halves[c]].bitcast(FP8X4),
                    rhs_scale=s_scales[g][:, halves[c]],
                    start=(g == 0),
                    stop=(g == 1),
                )
            accs[(i, c)] = acc

        def add_bias(i):
            vp = keep.tile([P, OUTF], F32, name="vp%d" % i, tag="vp%d" % i)
            if i in HALVED_FIRST:
                for c in range(2):
                    nc.vector.tensor_tensor(out=vp[:, halves[c]], in0=accs[(i, c)][:], in1=b1[:, halves[c]], op=ALU.add)
            else:
                nc.vector.tensor_tensor(out=vp[:], in0=accs[i][:], in1=b1[:], op=ALU.add)
            vps[i] = vp
            neg = keep.tile([P, OUTF], F32, name="neg%d" % i, tag="neg%d" % i)
            negs[i] = neg

        def clamp_vector(i):
            nc.vector.tensor_scalar(
                out=negs[i][:], in0=vps[i][:], scalar1=0.0, scalar2=-1.0, op0=ALU.max, op1=ALU.add
            )

        def exponent(i):
            ex = keep.tile([P, OUTF], F32, name="ex%d" % i, tag="ex%d" % i)
            for cols in pieces(i):
                nc.scalar.activation(out=ex[:, cols], in_=vps[i][:, cols], func=ACT.Exp)
            if i in MIN_ON_SCALAR:
                nc.scalar.activation(out=negs[i][:], in_=vps[i][:], func=ACT.Relu)
            exps[i] = ex

        def finish(i):
            res = keep.tile([P, OUTF], F32, name="res%d" % i, tag="res%d" % i)
            for cols in pieces(i):
                if i in MIN_ON_SCALAR:
                    nc.vector.scalar_tensor_tensor(
                        out=res[:, cols], in0=exps[i][:, cols], scalar=-1.0, in1=negs[i][:, cols], op0=ALU.add, op1=ALU.min
                    )
                else:
                    nc.vector.scalar_tensor_tensor(
                        out=res[:, cols], in0=exps[i][:, cols], scalar=1.0, in1=negs[i][:, cols], op0=ALU.min, op1=ALU.add
                    )
                nc.sync.dma_start(out=out[i * P : (i + 1) * P, cols], in_=res[:, cols])

        x_turn(0)
        x_turn(1)
        nc.tensor.matmul(
            out=bank_w[:, 0:P], lhsT=ident[:], rhs=x_raw[1][:, 1, :].bitcast(F32)[:, 0:P], start=True, stop=True
        )
        x_turn(2)
        x_turn(3)
        w_quant(0)
        x_copy(0)
        w_quant(1)
        x_quant(0)
        for u in range(1, 4):
            x_copy(u)
            x_quant(u)
        a_turn(0)
        a_square(0)
        s_multiply(0, 0)
        s_multiply_narrow(0)
        s_multiply_narrow(1)
        s_multiply(1, 0)
        s_multiply(1, 1)
        a_turn(1)
        s_copy(0, 0)
        s_copy_narrow(0)
        s_copy_narrow(1)
        s_copy(1, 0)
        s_copy(1, 1)
        for i in range(EARLY_TURNS, AHEAD + 1):
            a_turn(i)
        for i in range(EARLY_SQUARES, AHEAD):
            a_square(i)
        s_quant(0, 0)
        a_quant(0)
        s_quant(1, 0)
        multiply_half(0, 0)
        s_quant(0, 1)
        s_quant(1, 1)

        multiply_half(0, 1)
        a_quant(1)
        add_bias(0)
        a_quant(2)
        if 0 not in MIN_ON_SCALAR:
            clamp_vector(0)
        for j in range(NT + 1):
            if j + 1 in HALVED_FIRST:
                multiply_half(j + 1, 0)
                multiply_half(j + 1, 1)
            elif j + 1 < NT:
                multiply(j + 1)
            if j % 2 == 0 and j + AHEAD + 1 < NT:
                a_turn(j + AHEAD + 1)
                a_turn(j + AHEAD + 2)
            if j + AHEAD < NT:
                a_square(j + AHEAD)
            if j < NT:
                exponent(j)
            if AHEAD <= j + AHEAD - 1 < NT:
                a_quant(j + AHEAD - 1)
            if j + 1 < NT:
                add_bias(j + 1)
            if j >= 1:
                finish(j - 1)
            if j + 1 < NT and (j + 1) not in MIN_ON_SCALAR:
                clamp_vector(j + 1)
